import numpy as np
import ml_dtypes


def mxq(x, axis, fmt="e4m3"):
    dtype, down = {"e4m3": (ml_dtypes.float8_e4m3fn, 7), "e5m2": (ml_dtypes.float8_e5m2, 14)}[fmt]
    v = np.moveaxis(np.asarray(x, np.float32).astype(ml_dtypes.bfloat16).astype(np.float64), axis, -1)
    blocks = v.reshape(v.shape[:-1] + (-1, 32))
    amax = np.abs(blocks).max(-1, keepdims=True)
    byte = np.maximum(np.where(amax > 0, np.frexp(amax)[1] - 1 + 127, 0) - down, 1)
    scale = np.exp2(byte - 127.0)
    codes = (blocks / scale).astype(np.float32).astype(dtype).astype(np.float64)
    return np.moveaxis((codes * scale).reshape(v.shape), -1, axis)


WIDE = False


def mx_kscale(k):
    if not WIDE:
        return np.ones(k)
    levels = np.array([10, -10, 5, -5, 0])
    a = np.random.permutation(np.resize(levels, k // 512 * 4)).reshape(k // 512, 4)
    idx = np.arange(k)
    return np.exp2(a[idx // 512, idx % 128 // 32])


BF16 = ml_dtypes.bfloat16


def bf(x):
    return np.asarray(x, np.float32).astype(BF16)


def f64(x):
    return np.asarray(x).astype(np.float64)


N, C, H, W = 2, 512, 64, 64

REPARAM_OFFSET = 2.0 ** -18
PEDESTAL = REPARAM_OFFSET ** 2
BETA_MIN = 1e-6
BOUND_BETA = (BETA_MIN + PEDESTAL) ** 0.5
BOUND_GAMMA = PEDESTAL ** 0.5
INVERSE = False


def nn_reparam(v, bound):
    return np.square(np.maximum(v, bound)) - PEDESTAL


def setup_inputs():
    u = np.exp2(np.round(np.log2(mx_kscale(C)) / 2))
    amp = np.exp(0.5 * np.random.standard_normal((N, 1, H, W)))
    x = np.random.standard_normal((N, C, H, W)) * amp * u[None, :, None, None]
    beta = np.random.standard_normal(C) * u
    gamma = np.random.standard_normal((C, C)) * 1.5 / np.sqrt(C) * u[:, None] / u[None, :]
    return {"x": bf(x), "beta": bf(beta), "gamma": bf(gamma)}


def reference(x, beta, gamma):
    x = f64(x)
    beta_eff = nn_reparam(f64(beta), BOUND_BETA)
    gamma_eff = nn_reparam(f64(gamma), BOUND_GAMMA)
    x2 = x * x
    denom_sq = (mxq(gamma_eff, 1, "e4m3") @ mxq(x2, 1, "e4m3").reshape(N, C, H * W)).reshape(N, C, H, W)
    denom_sq = denom_sq + beta_eff[None, :, None, None]
    norm = np.sqrt(denom_sq) if INVERSE else 1.0 / np.sqrt(denom_sq)
    return x * norm

@@ -1,0 +1,180 @@
+import concourse.mybir as mybir
+from concourse.masks import make_identity
+
+FLOPS = 2 * 512 * 512 * 2 * 4096
+
+F32 = mybir.dt.float32
+BF16 = mybir.dt.bfloat16
+U32 = mybir.dt.uint32
+U8 = mybir.dt.uint8
+FP8X4 = mybir.dt.float8_e4m3fn_x4
+ALU = mybir.AluOpType
+ACT = mybir.ActivationFunctionType
+
+P = 128
+PACK = 4
+PIX = 4096
+CHUNK = 512
+N_CHUNKS = 2 * PIX // CHUNK
+S_COLS = 304
+
+PEDESTAL = 2.0 ** -36
+BOUND_GAMMA = 2.0 ** -18
+BOUND_BETA = (1e-6 + PEDESTAL) ** 0.5
+
+LOADS = ((0, 0, 512), (0, 512, 512), (0, 1024, 1024), (0, 2048, 2048), (1, 0, 2048), (1, 2048, 2048))
+
+
+def tile_einsumgdn_kernel(tc, x, beta, gamma, out):
+    nc = tc.nc
+    xv = x.rearrange("n (p j) h w -> n p j (h w)", j=PACK)
+    ov = out.rearrange("n (p j) h w -> n p j (h w)", j=PACK)
+
+    with tc.tile_pool(name="keep", bufs=1) as keep, tc.tile_pool(name="work", bufs=3) as work, tc.tile_pool(
+        name="res", bufs=6
+    ) as res, tc.psum_pool(name="psum", bufs=8) as psum, tc.manual_schedule():
+        x_tiles = []
+        for i, (n, p0, width) in enumerate(LOADS):
+            xt = keep.tile([P, PACK, width], BF16, name="x%d" % i, tag="x%d" % i)
+            x_tiles.append(xt)
+        g_sb = keep.tile([P, PACK * 512], BF16)
+        b_sb = keep.tile([P, PACK], BF16)
+
+        def load_x(i):
+            n, p0, width = LOADS[i]
+            nc.sync.dma_start(out=x_tiles[i][:], in_=xv[n, :, :, p0 : p0 + width])
+
+        load_x(0)
+        nc.sync.dma_start(out=g_sb[:], in_=gamma.rearrange("(m j) c -> m (j c)", j=PACK))
+        nc.sync.dma_start(out=b_sb[:], in_=beta.rearrange("(p j) -> p j", j=PACK))
+        for i in range(1, len(LOADS)):
+            load_x(i)
+
+        def where(k):
+            n = k // (PIX // CHUNK)
+            p0 = (k % (PIX // CHUNK)) * CHUNK
+            for i, (ln, lp, lw) in enumerate(LOADS):
+                if ln == n and lp <= p0 and p0 + CHUNK <= lp + lw:
+                    return x_tiles[i], p0 - lp, n, p0
+            raise ValueError("chunk outside the loads")
+
+        one = keep.tile([P, 1], F32)
+        nc.vector.memset(one[:], 1.0)
+        negb = keep.tile([P, 1], F32)
+        nc.vector.memset(negb[:], -BOUND_GAMMA)
+        warm = keep.tile([P, 1], F32)
+        nc.scalar.activation(out=warm[:], in_=one[:], func=ACT.Abs_reciprocal_sqrt)
+        ident = keep.tile([P, P], F32)
+        make_identity(nc, ident[:])
+
+        grouped = {}
+        codes = {}
+        planes = {}
+        results = {}
+
+        def square(k):
+            xt, off, n, p0 = where(k)
+            gq = work.tile([P, CHUNK, PACK], BF16, align_bytes=64, name="gq", tag="gq")
+            grouped[k] = gq
+
+            def views(w0, w1):
+                dst = gq[:, w0:w1, :].rearrange("p (c i) t -> p c t i", i=4)
+                src = xt[:, :, off + w0 : off + w1].rearrange("p t (c i) -> p c t i", i=4)
+                return dst, src
+
+            dst, src = views(0, S_COLS)
+            nc.scalar.activation(out=dst, in_=src, func=ACT.Square)
+            dst, src = views(S_COLS, CHUNK)
+            nc.vector.tensor_tensor(out=dst, in0=src, in1=src, op=ALU.mult)
+
+        def quantise(k):
+            cw = work.tile([P, CHUNK], U32, align_bytes=64, name="cw", tag="cw")
+            sp = work.tile([P, CHUNK], U8, align_bytes=64, name="sp", tag="sp")
+            codes[k] = cw
+            planes[k] = sp
+            nc.vector.quantize_mx(
+                out=cw[:].bitcast(FP8X4), scales=sp[:], in_=grouped[k][:].rearrange("p w t -> p (w t)")
+            )
+
+        square(0)
+        gw = g_sb[:].bitcast(F32)
+        a_sb = keep.tile([P, PACK * 512], F32)
+        for half in range(2):
+            tp = psum.tile([P, 512], F32, name="bank", tag="bank")
+            for jl in range(2):
+                jj = 2 * half + jl
+                for u in range(2):
+                    nc.tensor.transpose(
+                        tp[:, (2 * jl + u) * P : (2 * jl + u + 1) * P],
+                        gw[:, jj * 256 + u : (jj + 1) * 256 : 2],
+                        ident[:],
+                    )
+            tb = tp[:].bitcast(BF16)
+            for jl in range(2):
+                jj = 2 * half + jl
+                src = tb[:, jl * 512 : (jl + 1) * 512].rearrange("p (u m e) -> p m u e", u=2, e=2)
+                dst = a_sb[:, jj * 512 : (jj + 1) * 512].rearrange("p (m u e) -> p m u e", u=2, e=2)
+                if half == 0:
+                    nc.vector.tensor_scalar(
+                        out=dst, in0=src, scalar1=BOUND_GAMMA, scalar2=BOUND_GAMMA, op0=ALU.max, op1=ALU.subtract
+                    )
+                else:
+                    nc.scalar.activation(out=dst, in_=src, func=ACT.Relu, bias=negb[:], scale=1.0)
+        g_eff = keep.tile([P, PACK * 512], BF16, align_bytes=64)
+        nc.vector.scalar_tensor_tensor(
+            out=g_eff[:], in0=a_sb[:], scalar=2.0 * BOUND_GAMMA, in1=a_sb[:], op0=ALU.add, op1=ALU.mult
+        )
+        square(1)
+        g_codes = keep.tile([P, 512], U32, align_bytes=64)
+        g_plane = keep.tile([P, 512], U8, align_bytes=64)
+        nc.vector.quantize_mx(out=g_codes[:].bitcast(FP8X4), scales=g_plane[:], in_=g_eff[:])
+
+        b_max = keep.tile([P, PACK], F32)
+        nc.vector.tensor_scalar(out=b_max[:], in0=b_sb[:], scalar1=BOUND_BETA, scalar2=None, op0=ALU.max)
+        b_sq = keep.tile([P, PACK], F32)
+        nc.vector.tensor_tensor(out=b_sq[:], in0=b_max[:], in1=b_max[:], op=ALU.mult)
+        b_eff = keep.tile([P, PACK], F32)
+        nc.vector.tensor_scalar(out=b_eff[:], in0=b_sq[:], scalar1=PEDESTAL, scalar2=None, op0=ALU.subtract)
+
+        quantise(0)
+
+        def denominators(k):
+            r = res.tile([P, PACK, CHUNK], F32, name="r", tag="r")
+            results[k] = r
+            banks = []
+            for jj in range(PACK):
+                acc = psum.tile([P, CHUNK], F32, name="bank", tag="bank")
+                banks.append(acc)
+                nc.tensor.matmul_mx(
+                    out=acc[:],
+                    lhsT=g_codes[:, jj * P : (jj + 1) * P].bitcast(FP8X4),
+                    lhsT_scale=g_plane[:, jj * P : (jj + 1) * P],
+                    rhs=codes[k][:].bitcast(FP8X4),
+                    rhs_scale=planes[k][:],
+                    start=True,
+                    stop=True,
+                )
+            for jj in range(PACK):
+                nc.scalar.activation(
+                    out=r[:, jj, :],
+                    in_=banks[jj][:],
+                    func=ACT.Abs_reciprocal_sqrt,
+                    bias=b_eff[:, jj : jj + 1],
+                    scale=1.0,
+                )
+
+        def finish(k):
+            xt, off, n, p0 = where(k)
+            r = results[k]
+            nc.vector.tensor_tensor(out=r[:], in0=r[:], in1=xt[:, :, off : off + CHUNK], op=ALU.mult)
+            nc.sync.dma_start(out=ov[n, :, :, p0 : p0 + CHUNK], in_=r[:])
+
+        for k in range(N_CHUNKS):
+            if k + 2 < N_CHUNKS:
+                square(k + 2)
+            if k + 1 < N_CHUNKS:
+                quantise(k + 1)
+            denominators(k)
+            if k >= 1:
+                finish(k - 1)
+        finish(N_CHUNKS - 1)

@@ -16,13 +16,26 @@ PACK = 4
 PIX = 4096
 CHUNK = 512
 N_CHUNKS = 2 * PIX // CHUNK
-S_COLS = 304
+SQUARE_LEAD = 3
+QUANT_LEAD = 2
+FINE_CHUNKS = 4
+
+S_COLS = (256, 512, 512, 128, 256) + (320,) * 9 + (384, 384)
 
 PEDESTAL = 2.0 ** -36
 BOUND_GAMMA = 2.0 ** -18
 BOUND_BETA = (1e-6 + PEDESTAL) ** 0.5
 
-LOADS = ((0, 0, 512), (0, 512, 512), (0, 1024, 1024), (0, 2048, 2048), (1, 0, 2048), (1, 2048, 2048))
+LOADS = (
+    (0, 0, 512),
+    (0, 512, 512),
+    (0, 1024, 512),
+    (0, 1536, 512),
+    (0, 2048, 1024),
+    (0, 3072, 1024),
+    (1, 0, 2048),
+    (1, 2048, 2048),
+)
 
 
 def tile_einsumgdn_kernel(tc, x, beta, gamma, out):
@@ -30,7 +43,7 @@ def tile_einsumgdn_kernel(tc, x, beta, gamma, out):
     xv = x.rearrange("n (p j) h w -> n p j (h w)", j=PACK)
     ov = out.rearrange("n (p j) h w -> n p j (h w)", j=PACK)
 
-    with tc.tile_pool(name="keep", bufs=1) as keep, tc.tile_pool(name="work", bufs=3) as work, tc.tile_pool(
+    with tc.tile_pool(name="keep", bufs=1) as keep, tc.tile_pool(name="work", bufs=4) as work, tc.tile_pool(
         name="res", bufs=6
     ) as res, tc.psum_pool(name="psum", bufs=8) as psum, tc.manual_schedule():
         x_tiles = []
@@ -71,63 +84,40 @@ def tile_einsumgdn_kernel(tc, x, beta, gamma, out):
         codes = {}
         planes = {}
         results = {}
+        banks = {}
 
-        def square(k):
+        def square_views(k, w0, w1):
             xt, off, n, p0 = where(k)
-            gq = work.tile([P, CHUNK, PACK], BF16, align_bytes=64, name="gq", tag="gq")
-            grouped[k] = gq
+            if k not in grouped:
+                gq = work.tile([P, CHUNK, PACK], BF16, align_bytes=64, name="gq", tag="gq")
+                grouped[k] = gq
+            dst = grouped[k][:, w0:w1, :].rearrange("p (c i) t -> p c t i", i=4)
+            src = xt[:, :, off + w0 : off + w1].rearrange("p t (c i) -> p c t i", i=4)
+            return dst, src
 
-            def views(w0, w1):
-                dst = gq[:, w0:w1, :].rearrange("p (c i) t -> p c t i", i=4)
-                src = xt[:, :, off + w0 : off + w1].rearrange("p t (c i) -> p c t i", i=4)
-                return dst, src
+        def square_scalar(k):
+            if k < N_CHUNKS and S_COLS[k] > 0:
+                dst, src = square_views(k, 0, S_COLS[k])
+                nc.scalar.activation(out=dst, in_=src, func=ACT.Square)
 
-            dst, src = views(0, S_COLS)
-            nc.scalar.activation(out=dst, in_=src, func=ACT.Square)
-            dst, src = views(S_COLS, CHUNK)
-            nc.vector.tensor_tensor(out=dst, in0=src, in1=src, op=ALU.mult)
+        def square_vector(k):
+            if k < N_CHUNKS and S_COLS[k] < CHUNK:
+                dst, src = square_views(k, S_COLS[k], CHUNK)
+                nc.vector.tensor_tensor(out=dst, in0=src, in1=src, op=ALU.mult)
 
         def quantise(k):
-            cw = work.tile([P, CHUNK], U32, align_bytes=64, name="cw", tag="cw")
-            sp = work.tile([P, CHUNK], U8, align_bytes=64, name="sp", tag="sp")
+            if k >= N_CHUNKS:
+                return
+            cw = keep.tile([P, CHUNK], U32, align_bytes=64, name="cw%d" % k, tag="cw%d" % k)
+            sp = keep.tile([P, CHUNK], U8, align_bytes=64, name="sp%d" % k, tag="sp%d" % k)
             codes[k] = cw
             planes[k] = sp
             nc.vector.quantize_mx(
                 out=cw[:].bitcast(FP8X4), scales=sp[:], in_=grouped[k][:].rearrange("p w t -> p (w t)")
             )
 
-        square(0)
-        gw = g_sb[:].bitcast(F32)
-        a_sb = keep.tile([P, PACK * 512], F32)
-        for half in range(2):
-            tp = psum.tile([P, 512], F32, name="bank", tag="bank")
-            for jl in range(2):
-                jj = 2 * half + jl
-                for u in range(2):
-                    nc.tensor.transpose(
-                        tp[:, (2 * jl + u) * P : (2 * jl + u + 1) * P],
-                        gw[:, jj * 256 + u : (jj + 1) * 256 : 2],
-                        ident[:],
-                    )
-            tb = tp[:].bitcast(BF16)
-            for jl in range(2):
-                jj = 2 * half + jl
-                src = tb[:, jl * 512 : (jl + 1) * 512].rearrange("p (u m e) -> p m u e", u=2, e=2)
-                dst = a_sb[:, jj * 512 : (jj + 1) * 512].rearrange("p (m u e) -> p m u e", u=2, e=2)
-                if half == 0:
-                    nc.vector.tensor_scalar(
-                        out=dst, in0=src, scalar1=BOUND_GAMMA, scalar2=BOUND_GAMMA, op0=ALU.max, op1=ALU.subtract
-                    )
-                else:
-                    nc.scalar.activation(out=dst, in_=src, func=ACT.Relu, bias=negb[:], scale=1.0)
-        g_eff = keep.tile([P, PACK * 512], BF16, align_bytes=64)
-        nc.vector.scalar_tensor_tensor(
-            out=g_eff[:], in0=a_sb[:], scalar=2.0 * BOUND_GAMMA, in1=a_sb[:], op0=ALU.add, op1=ALU.mult
-        )
-        square(1)
-        g_codes = keep.tile([P, 512], U32, align_bytes=64)
-        g_plane = keep.tile([P, 512], U8, align_bytes=64)
-        nc.vector.quantize_mx(out=g_codes[:].bitcast(FP8X4), scales=g_plane[:], in_=g_eff[:])
+        square_scalar(0)
+        square_vector(0)
 
         b_max = keep.tile([P, PACK], F32)
         nc.vector.tensor_scalar(out=b_max[:], in0=b_sb[:], scalar1=BOUND_BETA, scalar2=None, op0=ALU.max)
@@ -138,13 +128,63 @@ def tile_einsumgdn_kernel(tc, x, beta, gamma, out):
 
         quantise(0)
 
-        def denominators(k):
+        gw = g_sb[:].bitcast(F32)
+        a_sb = keep.tile([P, PACK * 512], F32)
+        g_eff = keep.tile([P, PACK * 512], BF16, align_bytes=64)
+        t_banks = []
+        for half in range(2):
+            tp = psum.tile([P, 512], F32, name="bank", tag="bank")
+            t_banks.append(tp)
+            for jl in range(2):
+                jj = 2 * half + jl
+                for u in range(2):
+                    nc.tensor.transpose(
+                        tp[:, (2 * jl + u) * P : (2 * jl + u + 1) * P],
+                        gw[:, jj * 256 + u : (jj + 1) * 256 : 2],
+                        ident[:],
+                    )
+        for half in range(2):
+            tb = t_banks[half][:].bitcast(BF16)
+            for jl in range(2):
+                jj = 2 * half + jl
+                src = tb[:, jl * 512 : (jl + 1) * 512].rearrange("p (u m e) -> p m u e", u=2, e=2)
+                dst = a_sb[:, jj * 512 : (jj + 1) * 512].rearrange("p (m u e) -> p m u e", u=2, e=2)
+                if half == 0:
+                    nc.vector.tensor_scalar(
+                        out=dst, in0=src, scalar1=BOUND_GAMMA, scalar2=BOUND_GAMMA, op0=ALU.max, op1=ALU.subtract
+                    )
+                else:
+                    nc.scalar.activation(out=dst, in_=src, func=ACT.Relu, bias=negb[:], scale=1.0)
+        for half in range(2):
+            cols = slice(half * 1024, (half + 1) * 1024)
+            nc.vector.scalar_tensor_tensor(
+                out=g_eff[:, cols],
+                in0=a_sb[:, cols],
+                scalar=2.0 * BOUND_GAMMA,
+                in1=a_sb[:, cols],
+                op0=ALU.add,
+                op1=ALU.mult,
+            )
+        square_scalar(1)
+        square_scalar(2)
+        g_codes = keep.tile([P, 512], U32, align_bytes=64)
+        g_plane = keep.tile([P, 512], U8, align_bytes=64)
+        nc.vector.quantize_mx(out=g_codes[:].bitcast(FP8X4), scales=g_plane[:], in_=g_eff[:])
+        quantise(1)
+        square_vector(3)
+        square_scalar(3)
+        quantise(2)
+        square_vector(4)
+        squared_v = 4
+        squared_s = 3
+        quantised = 2
+
+        def passes(k):
             r = res.tile([P, PACK, CHUNK], F32, name="r", tag="r")
             results[k] = r
-            banks = []
             for jj in range(PACK):
                 acc = psum.tile([P, CHUNK], F32, name="bank", tag="bank")
-                banks.append(acc)
+                banks[(k, jj)] = acc
                 nc.tensor.matmul_mx(
                     out=acc[:],
                     lhsT=g_codes[:, jj * P : (jj + 1) * P].bitcast(FP8X4),
@@ -154,27 +194,50 @@ def tile_einsumgdn_kernel(tc, x, beta, gamma, out):
                     start=True,
                     stop=True,
                 )
-            for jj in range(PACK):
-                nc.scalar.activation(
-                    out=r[:, jj, :],
-                    in_=banks[jj][:],
-                    func=ACT.Abs_reciprocal_sqrt,
-                    bias=b_eff[:, jj : jj + 1],
-                    scale=1.0,
-                )
 
-        def finish(k):
+        def rsqrt(k, jj):
+            nc.scalar.activation(
+                out=results[k][:, jj, :],
+                in_=banks[(k, jj)][:],
+                func=ACT.Abs_reciprocal_sqrt,
+                bias=b_eff[:, jj : jj + 1],
+                scale=1.0,
+            )
+
+        def product(k, j0, j1):
             xt, off, n, p0 = where(k)
             r = results[k]
-            nc.vector.tensor_tensor(out=r[:], in0=r[:], in1=xt[:, :, off : off + CHUNK], op=ALU.mult)
-            nc.sync.dma_start(out=ov[n, :, :, p0 : p0 + CHUNK], in_=r[:])
+            nc.vector.tensor_tensor(
+                out=r[:, j0:j1, :], in0=r[:, j0:j1, :], in1=xt[:, j0:j1, off : off + CHUNK], op=ALU.mult
+            )
+
+        def store(k, j0, j1):
+            xt, off, n, p0 = where(k)
+            nc.sync.dma_start(out=ov[n, :, j0:j1, p0 : p0 + CHUNK], in_=results[k][:, j0:j1, :])
 
         for k in range(N_CHUNKS):
-            if k + 2 < N_CHUNKS:
-                square(k + 2)
-            if k + 1 < N_CHUNKS:
-                quantise(k + 1)
-            denominators(k)
-            if k >= 1:
-                finish(k - 1)
-        finish(N_CHUNKS - 1)
+            fine = k >= N_CHUNKS - FINE_CHUNKS
+            passes(k)
+            rsqrt(k, 0)
+            rsqrt(k, 1)
+            if k + SQUARE_LEAD > squared_s:
+                square_scalar(k + SQUARE_LEAD)
+            rsqrt(k, 2)
+            rsqrt(k, 3)
+            if fine:
+                for jj in (0, 1):
+                    product(k, jj, jj + 1)
+                    store(k, jj, jj + 1)
+            else:
+                product(k, 0, 2)
+            if k + QUANT_LEAD > quantised:
+                quantise(k + QUANT_LEAD)
+            if k + SQUARE_LEAD > squared_v:
+                square_vector(k + SQUARE_LEAD)
+            if fine:
+                for jj in (2, 3):
+                    product(k, jj, jj + 1)
+                    store(k, jj, jj + 1)
+            else:
+                product(k, 2, 4)
+                store(k, 0, 4)

@@ -18,9 +18,11 @@ CHUNK = 512
 N_CHUNKS = 2 * PIX // CHUNK
 SQUARE_LEAD = 3
 QUANT_LEAD = 2
-FINE_CHUNKS = 4
+FINE_CHUNKS = 3
+XP = 192
+G_COLS = 128
 
-S_COLS = (256, 512, 512, 128, 256) + (320,) * 9 + (384, 384)
+S_COLS = (256, 320, 320, 224, 256, 240, 288, 240, 240, 240, 272, 264, 240, 240, 320, 280)
 
 PEDESTAL = 2.0 ** -36
 BOUND_GAMMA = 2.0 ** -18
@@ -43,9 +45,9 @@ def tile_einsumgdn_kernel(tc, x, beta, gamma, out):
     xv = x.rearrange("n (p j) h w -> n p j (h w)", j=PACK)
     ov = out.rearrange("n (p j) h w -> n p j (h w)", j=PACK)
 
-    with tc.tile_pool(name="keep", bufs=1) as keep, tc.tile_pool(name="work", bufs=4) as work, tc.tile_pool(
+    with tc.tile_pool(name="keep", bufs=1) as keep, tc.tile_pool(name="work", bufs=6) as work, tc.tile_pool(
         name="res", bufs=6
-    ) as res, tc.psum_pool(name="psum", bufs=8) as psum, tc.manual_schedule():
+    ) as res, tc.psum_pool(name="psum", bufs=4) as psum, tc.manual_schedule():
         x_tiles = []
         for i, (n, p0, width) in enumerate(LOADS):
             xt = keep.tile([P, PACK, width], BF16, name="x%d" % i, tag="x%d" % i)
@@ -77,6 +79,8 @@ def tile_einsumgdn_kernel(tc, x, beta, gamma, out):
         nc.vector.memset(negb[:], -BOUND_GAMMA)
         warm = keep.tile([P, 1], F32)
         nc.scalar.activation(out=warm[:], in_=one[:], func=ACT.Abs_reciprocal_sqrt)
+        ident_bf = keep.tile([P, P], BF16)
+        make_identity(nc, ident_bf[:])
         ident = keep.tile([P, P], F32)
         make_identity(nc, ident[:])
 
@@ -85,6 +89,18 @@ def tile_einsumgdn_kernel(tc, x, beta, gamma, out):
         planes = {}
         results = {}
         banks = {}
+        x_psum = {}
+
+        def copy_to_psum(k):
+            if k >= N_CHUNKS:
+                return
+            xt, off, n, p0 = where(k)
+            xp = psum.tile([P, PACK, 256], BF16, name="xp", tag="xp")
+            x_psum[k] = xp
+            for jj in range(PACK):
+                nc.tensor.matmul(
+                    out=xp[:, jj, 0:XP], lhsT=ident_bf[:], rhs=xt[:, jj, off : off + XP], start=True, stop=True
+                )
 
         def square_views(k, w0, w1):
             xt, off, n, p0 = where(k)
@@ -96,14 +112,20 @@ def tile_einsumgdn_kernel(tc, x, beta, gamma, out):
             return dst, src
 
         def square_scalar(k):
-            if k < N_CHUNKS and S_COLS[k] > 0:
-                dst, src = square_views(k, 0, S_COLS[k])
+            if k < N_CHUNKS:
+                dst, src = square_views(k, CHUNK - S_COLS[k], CHUNK)
                 nc.scalar.activation(out=dst, in_=src, func=ACT.Square)
 
         def square_vector(k):
-            if k < N_CHUNKS and S_COLS[k] < CHUNK:
-                dst, src = square_views(k, S_COLS[k], CHUNK)
+            if k < N_CHUNKS and XP + S_COLS[k] < CHUNK:
+                dst, src = square_views(k, XP, CHUNK - S_COLS[k])
                 nc.vector.tensor_tensor(out=dst, in0=src, in1=src, op=ALU.mult)
+
+        def square_psum(k):
+            if k < N_CHUNKS:
+                dst, src = square_views(k, 0, XP)
+                src_psum = x_psum[k][:, :, 0:XP].rearrange("p t (c i) -> p c t i", i=4)
+                nc.vector.tensor_tensor(out=dst, in0=src_psum, in1=src, op=ALU.mult)
 
         def quantise(k):
             if k >= N_CHUNKS:
@@ -116,17 +138,26 @@ def tile_einsumgdn_kernel(tc, x, beta, gamma, out):
                 out=cw[:].bitcast(FP8X4), scales=sp[:], in_=grouped[k][:].rearrange("p w t -> p (w t)")
             )
 
+        def passes(k):
+            if k >= N_CHUNKS:
+                return
+            for jj in range(PACK):
+                acc = psum.tile([P, CHUNK], F32, name="bank", tag="bank")
+                banks[(k, jj)] = acc
+                nc.tensor.matmul_mx(
+                    out=acc[:],
+                    lhsT=g_codes[:, jj * P : (jj + 1) * P].bitcast(FP8X4),
+                    lhsT_scale=g_plane[:, jj * P : (jj + 1) * P],
+                    rhs=codes[k][:].bitcast(FP8X4),
+                    rhs_scale=planes[k][:],
+                    start=True,
+                    stop=True,
+                )
+
+        copy_to_psum(0)
         square_scalar(0)
         square_vector(0)
-
-        b_max = keep.tile([P, PACK], F32)
-        nc.vector.tensor_scalar(out=b_max[:], in0=b_sb[:], scalar1=BOUND_BETA, scalar2=None, op0=ALU.max)
-        b_sq = keep.tile([P, PACK], F32)
-        nc.vector.tensor_tensor(out=b_sq[:], in0=b_max[:], in1=b_max[:], op=ALU.mult)
-        b_eff = keep.tile([P, PACK], F32)
-        nc.vector.tensor_scalar(out=b_eff[:], in0=b_sq[:], scalar1=PEDESTAL, scalar2=None, op0=ALU.subtract)
-
-        quantise(0)
+        square_psum(0)
 
         gw = g_sb[:].bitcast(F32)
         a_sb = keep.tile([P, PACK * 512], F32)
@@ -143,6 +174,18 @@ def tile_einsumgdn_kernel(tc, x, beta, gamma, out):
                         gw[:, jj * 256 + u : (jj + 1) * 256 : 2],
                         ident[:],
                     )
+        copy_to_psum(1)
+        copy_to_psum(2)
+
+        b_max = keep.tile([P, PACK], F32)
+        nc.vector.tensor_scalar(out=b_max[:], in0=b_sb[:], scalar1=BOUND_BETA, scalar2=None, op0=ALU.max)
+        b_sq = keep.tile([P, PACK], F32)
+        nc.vector.tensor_tensor(out=b_sq[:], in0=b_max[:], in1=b_max[:], op=ALU.mult)
+        b_eff = keep.tile([P, PACK], F32)
+        nc.vector.tensor_scalar(out=b_eff[:], in0=b_sq[:], scalar1=PEDESTAL, scalar2=None, op0=ALU.subtract)
+
+        quantise(0)
+
         for half in range(2):
             tb = t_banks[half][:].bitcast(BF16)
             for jl in range(2):
@@ -166,36 +209,21 @@ def tile_einsumgdn_kernel(tc, x, beta, gamma, out):
                 op1=ALU.mult,
             )
         square_scalar(1)
-        square_scalar(2)
         g_codes = keep.tile([P, 512], U32, align_bytes=64)
         g_plane = keep.tile([P, 512], U8, align_bytes=64)
         nc.vector.quantize_mx(out=g_codes[:].bitcast(FP8X4), scales=g_plane[:], in_=g_eff[:])
+        passes(0)
+        square_scalar(2)
+        square_vector(1)
+        square_psum(1)
         quantise(1)
-        square_vector(3)
-        square_scalar(3)
-        quantise(2)
-        square_vector(4)
-        squared_v = 4
-        squared_s = 3
-        quantised = 2
-
-        def passes(k):
-            r = res.tile([P, PACK, CHUNK], F32, name="r", tag="r")
-            results[k] = r
-            for jj in range(PACK):
-                acc = psum.tile([P, CHUNK], F32, name="bank", tag="bank")
-                banks[(k, jj)] = acc
-                nc.tensor.matmul_mx(
-                    out=acc[:],
-                    lhsT=g_codes[:, jj * P : (jj + 1) * P].bitcast(FP8X4),
-                    lhsT_scale=g_plane[:, jj * P : (jj + 1) * P],
-                    rhs=codes[k][:].bitcast(FP8X4),
-                    rhs_scale=planes[k][:],
-                    start=True,
-                    stop=True,
-                )
+        square_vector(2)
+        square_psum(2)
 
         def rsqrt(k, jj):
+            if jj == 0:
+                r = res.tile([P, PACK, CHUNK], F32, name="r", tag="r")
+                results[k] = r
             nc.scalar.activation(
                 out=results[k][:, jj, :],
                 in_=banks[(k, jj)][:],
@@ -204,40 +232,39 @@ def tile_einsumgdn_kernel(tc, x, beta, gamma, out):
                 scale=1.0,
             )
 
-        def product(k, j0, j1):
+        def product(engine, k, j0, j1, w0, w1):
             xt, off, n, p0 = where(k)
-            r = results[k]
-            nc.vector.tensor_tensor(
-                out=r[:, j0:j1, :], in0=r[:, j0:j1, :], in1=xt[:, j0:j1, off : off + CHUNK], op=ALU.mult
-            )
+            r = results[k][:, j0:j1, w0:w1]
+            engine.tensor_tensor(out=r, in0=r, in1=xt[:, j0:j1, off + w0 : off + w1], op=ALU.mult)
+
+        def product_psum(k):
+            r = results[k][:, :, 0:XP]
+            nc.vector.tensor_tensor(out=r, in0=x_psum[k][:, :, 0:XP], in1=r, op=ALU.mult)
 
         def store(k, j0, j1):
             xt, off, n, p0 = where(k)
             nc.sync.dma_start(out=ov[n, :, j0:j1, p0 : p0 + CHUNK], in_=results[k][:, j0:j1, :])
 
         for k in range(N_CHUNKS):
-            fine = k >= N_CHUNKS - FINE_CHUNKS
-            passes(k)
-            rsqrt(k, 0)
-            rsqrt(k, 1)
-            if k + SQUARE_LEAD > squared_s:
+            if k >= N_CHUNKS - FINE_CHUNKS:
+                for jj in range(PACK):
+                    rsqrt(k, jj)
+                    product(nc.vector, k, jj, jj + 1, 0, CHUNK)
+                    store(k, jj, jj + 1)
+                    if jj == 1:
+                        quantise(k + QUANT_LEAD)
+                passes(k + 1)
+            else:
+                for jj in range(PACK):
+                    rsqrt(k, jj)
+                passes(k + 1)
+                copy_to_psum(k + SQUARE_LEAD)
                 square_scalar(k + SQUARE_LEAD)
-            rsqrt(k, 2)
-            rsqrt(k, 3)
-            if fine:
-                for jj in (0, 1):
-                    product(k, jj, jj + 1)
-                    store(k, jj, jj + 1)
-            else:
-                product(k, 0, 2)
-            if k + QUANT_LEAD > quantised:
+                product(nc.vector, k, 0, 2, XP, CHUNK - G_COLS)
                 quantise(k + QUANT_LEAD)
-            if k + SQUARE_LEAD > squared_v:
+                product(nc.vector, k, 2, 4, XP, CHUNK - G_COLS)
+                product(nc.gpsimd, k, 0, 4, CHUNK - G_COLS, CHUNK)
+                product_psum(k)
+                square_psum(k + SQUARE_LEAD)
                 square_vector(k + SQUARE_LEAD)
-            if fine:
-                for jj in (2, 3):
-                    product(k, jj, jj + 1)
-                    store(k, jj, jj + 1)
-            else:
-                product(k, 2, 4)
                 store(k, 0, 4)

@@ -18,11 +18,11 @@ CHUNK = 512
 N_CHUNKS = 2 * PIX // CHUNK
 SQUARE_LEAD = 3
 QUANT_LEAD = 2
-FINE_CHUNKS = 3
+FINE_CHUNKS = 4
 XP = 192
-G_COLS = 128
+G_COLS = 144
 
-S_COLS = (256, 320, 320, 224, 256, 240, 288, 240, 240, 240, 272, 264, 240, 240, 320, 280)
+S_COLS = (320,) * 3 + (264,) * 10 + (320,) * 3
 
 PEDESTAL = 2.0 ** -36
 BOUND_GAMMA = 2.0 ** -18
@@ -246,6 +246,7 @@ def tile_einsumgdn_kernel(tc, x, beta, gamma, out):
             nc.sync.dma_start(out=ov[n, :, j0:j1, p0 : p0 + CHUNK], in_=results[k][:, j0:j1, :])
 
         for k in range(N_CHUNKS):
+            copy_to_psum(k + SQUARE_LEAD)
             if k >= N_CHUNKS - FINE_CHUNKS:
                 for jj in range(PACK):
                     rsqrt(k, jj)
@@ -254,11 +255,13 @@ def tile_einsumgdn_kernel(tc, x, beta, gamma, out):
                     if jj == 1:
                         quantise(k + QUANT_LEAD)
                 passes(k + 1)
+                square_scalar(k + SQUARE_LEAD)
+                square_psum(k + SQUARE_LEAD)
+                square_vector(k + SQUARE_LEAD)
             else:
                 for jj in range(PACK):
                     rsqrt(k, jj)
                 passes(k + 1)
-                copy_to_psum(k + SQUARE_LEAD)
                 square_scalar(k + SQUARE_LEAD)
                 product(nc.vector, k, 0, 2, XP, CHUNK - G_COLS)
                 quantise(k + QUANT_LEAD)

@@ -156,8 +156,8 @@ def tile_einsumgdn_kernel(tc, x, beta, gamma, out):
 
         copy_to_psum(0)
         square_scalar(0)
-        square_vector(0)
-        square_psum(0)
+        dst0, src0 = square_views(0, 0, CHUNK - S_COLS[0])
+        nc.vector.tensor_tensor(out=dst0, in0=src0, in1=src0, op=ALU.mult)
 
         gw = g_sb[:].bitcast(F32)
         a_sb = keep.tile([P, PACK * 512], F32)
@@ -178,11 +178,11 @@ def tile_einsumgdn_kernel(tc, x, beta, gamma, out):
         copy_to_psum(2)
 
         b_max = keep.tile([P, PACK], F32)
-        nc.vector.tensor_scalar(out=b_max[:], in0=b_sb[:], scalar1=BOUND_BETA, scalar2=None, op0=ALU.max)
+        nc.gpsimd.tensor_scalar(out=b_max[:], in0=b_sb[:], scalar1=BOUND_BETA, scalar2=None, op0=ALU.max)
         b_sq = keep.tile([P, PACK], F32)
-        nc.vector.tensor_tensor(out=b_sq[:], in0=b_max[:], in1=b_max[:], op=ALU.mult)
+        nc.gpsimd.tensor_tensor(out=b_sq[:], in0=b_max[:], in1=b_max[:], op=ALU.mult)
         b_eff = keep.tile([P, PACK], F32)
-        nc.vector.tensor_scalar(out=b_eff[:], in0=b_sq[:], scalar1=PEDESTAL, scalar2=None, op0=ALU.subtract)
+        nc.gpsimd.tensor_scalar(out=b_eff[:], in0=b_sq[:], scalar1=PEDESTAL, scalar2=None, op0=ALU.subtract)
 
         quantise(0)
 
@@ -220,13 +220,13 @@ def tile_einsumgdn_kernel(tc, x, beta, gamma, out):
         square_vector(2)
         square_psum(2)
 
-        def rsqrt(k, jj):
+        def rsqrt(k, jj, w0=0, w1=CHUNK):
             if jj == 0:
                 r = res.tile([P, PACK, CHUNK], F32, name="r", tag="r")
                 results[k] = r
             nc.scalar.activation(
-                out=results[k][:, jj, :],
-                in_=banks[(k, jj)][:],
+                out=results[k][:, jj, w0:w1],
+                in_=banks[(k, jj)][:, w0:w1],
                 func=ACT.Abs_reciprocal_sqrt,
                 bias=b_eff[:, jj : jj + 1],
                 scale=1.0,
@@ -241,17 +241,19 @@ def tile_einsumgdn_kernel(tc, x, beta, gamma, out):
             r = results[k][:, :, 0:XP]
             nc.vector.tensor_tensor(out=r, in0=x_psum[k][:, :, 0:XP], in1=r, op=ALU.mult)
 
-        def store(k, j0, j1):
+        def store(k, j0, j1, w0=0, w1=CHUNK):
             xt, off, n, p0 = where(k)
-            nc.sync.dma_start(out=ov[n, :, j0:j1, p0 : p0 + CHUNK], in_=results[k][:, j0:j1, :])
+            nc.sync.dma_start(out=ov[n, :, j0:j1, p0 + w0 : p0 + w1], in_=results[k][:, j0:j1, w0:w1])
 
         for k in range(N_CHUNKS):
             copy_to_psum(k + SQUARE_LEAD)
             if k >= N_CHUNKS - FINE_CHUNKS:
                 for jj in range(PACK):
-                    rsqrt(k, jj)
-                    product(nc.vector, k, jj, jj + 1, 0, CHUNK)
-                    store(k, jj, jj + 1)
+                    last = k == N_CHUNKS - 1 and jj == PACK - 1
+                    for w0, w1 in ((0, 256), (256, CHUNK)) if last else ((0, CHUNK),):
+                        rsqrt(k, jj, w0, w1)
+                        product(nc.vector, k, jj, jj + 1, w0, w1)
+                        store(k, jj, jj + 1, w0, w1)
                     if jj == 1:
                         quantise(k + QUANT_LEAD)
                 passes(k + 1)

@@ -22,7 +22,7 @@ FINE_CHUNKS = 4
 XP = 192
 G_COLS = 144
 
-S_COLS = (320,) * 3 + (264,) * 10 + (320,) * 3
+S_COLS = (320,) * 3 + (248,) * 10 + (320,) * 3
 
 PEDESTAL = 2.0 ** -36
 BOUND_GAMMA = 2.0 ** -18

@@ -17,12 +17,13 @@ PIX = 4096
 CHUNK = 512
 N_CHUNKS = 2 * PIX // CHUNK
 SQUARE_LEAD = 3
+S_LEAD = 4
 QUANT_LEAD = 2
 FINE_CHUNKS = 4
-XP = 192
-G_COLS = 144
+XP = 216
+G_COLS = 168
 
-S_COLS = (320,) * 3 + (248,) * 10 + (320,) * 3
+S_COLS = (296,) * 3 + (228,) * 10 + (296, 296, 512)
 
 PEDESTAL = 2.0 ** -36
 BOUND_GAMMA = 2.0 ** -18
@@ -92,7 +93,7 @@ def tile_einsumgdn_kernel(tc, x, beta, gamma, out):
         x_psum = {}
 
         def copy_to_psum(k):
-            if k >= N_CHUNKS:
+            if k >= N_CHUNKS or S_COLS[k] == CHUNK:
                 return
             xt, off, n, p0 = where(k)
             xp = psum.tile([P, PACK, 256], BF16, name="xp", tag="xp")
@@ -122,7 +123,7 @@ def tile_einsumgdn_kernel(tc, x, beta, gamma, out):
                 nc.vector.tensor_tensor(out=dst, in0=src, in1=src, op=ALU.mult)
 
         def square_psum(k):
-            if k < N_CHUNKS:
+            if k < N_CHUNKS and S_COLS[k] < CHUNK:
                 dst, src = square_views(k, 0, XP)
                 src_psum = x_psum[k][:, :, 0:XP].rearrange("p t (c i) -> p c t i", i=4)
                 nc.vector.tensor_tensor(out=dst, in0=src_psum, in1=src, op=ALU.mult)
@@ -214,6 +215,7 @@ def tile_einsumgdn_kernel(tc, x, beta, gamma, out):
         nc.vector.quantize_mx(out=g_codes[:].bitcast(FP8X4), scales=g_plane[:], in_=g_eff[:])
         passes(0)
         square_scalar(2)
+        square_scalar(3)
         square_vector(1)
         square_psum(1)
         quantise(1)
@@ -254,17 +256,15 @@ def tile_einsumgdn_kernel(tc, x, beta, gamma, out):
                         rsqrt(k, jj, w0, w1)
                         product(nc.vector, k, jj, jj + 1, w0, w1)
                         store(k, jj, jj + 1, w0, w1)
-                    if jj == 1:
-                        quantise(k + QUANT_LEAD)
                 passes(k + 1)
-                square_scalar(k + SQUARE_LEAD)
+                square_scalar(k + S_LEAD)
                 square_psum(k + SQUARE_LEAD)
                 square_vector(k + SQUARE_LEAD)
             else:
                 for jj in range(PACK):
                     rsqrt(k, jj)
                 passes(k + 1)
-                square_scalar(k + SQUARE_LEAD)
+                square_scalar(k + S_LEAD)
                 product(nc.vector, k, 0, 2, XP, CHUNK - G_COLS)
                 quantise(k + QUANT_LEAD)
                 product(nc.vector, k, 2, 4, XP, CHUNK - G_COLS)
@@ -273,3 +273,6 @@ def tile_einsumgdn_kernel(tc, x, beta, gamma, out):
                 square_psum(k + SQUARE_LEAD)
                 square_vector(k + SQUARE_LEAD)
                 store(k, 0, 4)
+                if k == N_CHUNKS - FINE_CHUNKS - 1:
+                    for late in range(k + QUANT_LEAD + 1, N_CHUNKS):
+                        quantise(late)

@@ -20,6 +20,7 @@ SQUARE_LEAD = 3
 S_LEAD = 4
 QUANT_LEAD = 2
 FINE_CHUNKS = 4
+COARSE = N_CHUNKS - FINE_CHUNKS
 XP = 216
 G_COLS = 168
 
@@ -48,7 +49,7 @@ def tile_einsumgdn_kernel(tc, x, beta, gamma, out):
 
     with tc.tile_pool(name="keep", bufs=1) as keep, tc.tile_pool(name="work", bufs=6) as work, tc.tile_pool(
         name="res", bufs=6
-    ) as res, tc.psum_pool(name="psum", bufs=4) as psum, tc.manual_schedule():
+    ) as res, tc.tile_pool(name="res2", bufs=2) as res2, tc.psum_pool(name="psum", bufs=4) as psum, tc.manual_schedule():
         x_tiles = []
         for i, (n, p0, width) in enumerate(LOADS):
             xt = keep.tile([P, PACK, width], BF16, name="x%d" % i, tag="x%d" % i)
@@ -89,6 +90,7 @@ def tile_einsumgdn_kernel(tc, x, beta, gamma, out):
         codes = {}
         planes = {}
         results = {}
+        pairs = {}
         banks = {}
         x_psum = {}
 
@@ -139,21 +141,22 @@ def tile_einsumgdn_kernel(tc, x, beta, gamma, out):
                 out=cw[:].bitcast(FP8X4), scales=sp[:], in_=grouped[k][:].rearrange("p w t -> p (w t)")
             )
 
+        def pass_one(k, jj):
+            acc = psum.tile([P, CHUNK], F32, name="bank", tag="bank")
+            banks[(k, jj)] = acc
+            nc.tensor.matmul_mx(
+                out=acc[:],
+                lhsT=g_codes[:, jj * P : (jj + 1) * P].bitcast(FP8X4),
+                lhsT_scale=g_plane[:, jj * P : (jj + 1) * P],
+                rhs=codes[k][:].bitcast(FP8X4),
+                rhs_scale=planes[k][:],
+                start=True,
+                stop=True,
+            )
+
         def passes(k):
-            if k >= N_CHUNKS:
-                return
             for jj in range(PACK):
-                acc = psum.tile([P, CHUNK], F32, name="bank", tag="bank")
-                banks[(k, jj)] = acc
-                nc.tensor.matmul_mx(
-                    out=acc[:],
-                    lhsT=g_codes[:, jj * P : (jj + 1) * P].bitcast(FP8X4),
-                    lhsT_scale=g_plane[:, jj * P : (jj + 1) * P],
-                    rhs=codes[k][:].bitcast(FP8X4),
-                    rhs_scale=planes[k][:],
-                    start=True,
-                    stop=True,
-                )
+                pass_one(k, jj)
 
         copy_to_psum(0)
         square_scalar(0)
@@ -223,9 +226,14 @@ def tile_einsumgdn_kernel(tc, x, beta, gamma, out):
         square_psum(2)
 
         def rsqrt(k, jj, w0=0, w1=CHUNK):
-            if jj == 0:
+            if jj == 0 and k < COARSE:
                 r = res.tile([P, PACK, CHUNK], F32, name="r", tag="r")
                 results[k] = r
+            if jj == 0 and k >= COARSE and k % 2 == 0:
+                two = res2.tile([P, PACK, 2 * CHUNK], F32, name="two", tag="two")
+                pairs[k] = two
+                results[k] = two[:, :, 0:CHUNK]
+                results[k + 1] = two[:, :, CHUNK : 2 * CHUNK]
             nc.scalar.activation(
                 out=results[k][:, jj, w0:w1],
                 in_=banks[(k, jj)][:, w0:w1],
@@ -247,32 +255,43 @@ def tile_einsumgdn_kernel(tc, x, beta, gamma, out):
             xt, off, n, p0 = where(k)
             nc.sync.dma_start(out=ov[n, :, j0:j1, p0 + w0 : p0 + w1], in_=results[k][:, j0:j1, w0:w1])
 
-        for k in range(N_CHUNKS):
+        def product_two(k, jj):
+            xt, off, n, p0 = where(k)
+            r = pairs[k][:, jj, :]
+            nc.vector.tensor_tensor(out=r, in0=r, in1=xt[:, jj, off : off + 2 * CHUNK], op=ALU.mult)
+            nc.sync.dma_start(out=ov[n, :, jj, p0 : p0 + 2 * CHUNK], in_=r)
+
+        units = [(first + h, jj) for first in range(COARSE, N_CHUNKS, 2) for jj in range(PACK) for h in (0, 1)]
+
+        for k in range(COARSE):
             copy_to_psum(k + SQUARE_LEAD)
-            if k >= N_CHUNKS - FINE_CHUNKS:
-                for jj in range(PACK):
-                    last = k == N_CHUNKS - 1 and jj == PACK - 1
-                    for w0, w1 in ((0, 256), (256, CHUNK)) if last else ((0, CHUNK),):
-                        rsqrt(k, jj, w0, w1)
-                        product(nc.vector, k, jj, jj + 1, w0, w1)
-                        store(k, jj, jj + 1, w0, w1)
+            for jj in range(PACK):
+                rsqrt(k, jj)
+            if k + 1 < COARSE:
                 passes(k + 1)
-                square_scalar(k + S_LEAD)
-                square_psum(k + SQUARE_LEAD)
-                square_vector(k + SQUARE_LEAD)
-            else:
-                for jj in range(PACK):
-                    rsqrt(k, jj)
-                passes(k + 1)
-                square_scalar(k + S_LEAD)
-                product(nc.vector, k, 0, 2, XP, CHUNK - G_COLS)
-                quantise(k + QUANT_LEAD)
-                product(nc.vector, k, 2, 4, XP, CHUNK - G_COLS)
-                product(nc.gpsimd, k, 0, 4, CHUNK - G_COLS, CHUNK)
-                product_psum(k)
-                square_psum(k + SQUARE_LEAD)
-                square_vector(k + SQUARE_LEAD)
-                store(k, 0, 4)
-                if k == N_CHUNKS - FINE_CHUNKS - 1:
-                    for late in range(k + QUANT_LEAD + 1, N_CHUNKS):
-                        quantise(late)
+            square_scalar(k + S_LEAD)
+            product(nc.vector, k, 0, 2, XP, CHUNK - G_COLS)
+            quantise(k + QUANT_LEAD)
+            if k + 1 == COARSE:
+                for unit in units[0:4]:
+                    pass_one(unit[0], unit[1])
+            product(nc.vector, k, 2, 4, XP, CHUNK - G_COLS)
+            product(nc.gpsimd, k, 0, 4, CHUNK - G_COLS, CHUNK)
+            product_psum(k)
+            square_psum(k + SQUARE_LEAD)
+            square_vector(k + SQUARE_LEAD)
+            store(k, 0, 4)
+        for late in range(COARSE + QUANT_LEAD, N_CHUNKS):
+            quantise(late)
+
+        for i, (k, jj) in enumerate(units):
+            end = k >= N_CHUNKS - 2 and jj == PACK - 1
+            for w0, w1 in ((0, 256), (256, CHUNK)) if i == len(units) - 1 else ((0, CHUNK),):
+                rsqrt(k, jj, w0, w1)
+                if end:
+                    product(nc.vector, k, jj, jj + 1, w0, w1)
+                    store(k, jj, jj + 1, w0, w1)
+            if i + 4 < len(units):
+                pass_one(units[i + 4][0], units[i + 4][1])
+            if k % 2 == 1 and not end:
+                product_two(k - 1, jj)

@@ -167,17 +167,15 @@ def tile_einsumgdn_kernel(tc, x, beta, gamma, out):
         a_sb = keep.tile([P, PACK * 512], F32)
         g_eff = keep.tile([P, PACK * 512], BF16, align_bytes=64)
         t_banks = []
-        for half in range(2):
+        for jj in range(PACK):
             tp = psum.tile([P, 512], F32, name="bank", tag="bank")
             t_banks.append(tp)
-            for jl in range(2):
-                jj = 2 * half + jl
-                for u in range(2):
-                    nc.tensor.transpose(
-                        tp[:, (2 * jl + u) * P : (2 * jl + u + 1) * P],
-                        gw[:, jj * 256 + u : (jj + 1) * 256 : 2],
-                        ident[:],
-                    )
+            for u in range(2):
+                nc.tensor.transpose(
+                    tp[:, u * P : (u + 1) * P],
+                    gw[:, jj * 256 + u : (jj + 1) * 256 : 2],
+                    ident[:],
+                )
         copy_to_psum(1)
         copy_to_psum(2)
 
@@ -190,18 +188,16 @@ def tile_einsumgdn_kernel(tc, x, beta, gamma, out):
 
         quantise(0)
 
-        for half in range(2):
-            tb = t_banks[half][:].bitcast(BF16)
-            for jl in range(2):
-                jj = 2 * half + jl
-                src = tb[:, jl * 512 : (jl + 1) * 512].rearrange("p (u m e) -> p m u e", u=2, e=2)
-                dst = a_sb[:, jj * 512 : (jj + 1) * 512].rearrange("p (m u e) -> p m u e", u=2, e=2)
-                if half == 0:
-                    nc.vector.tensor_scalar(
-                        out=dst, in0=src, scalar1=BOUND_GAMMA, scalar2=BOUND_GAMMA, op0=ALU.max, op1=ALU.subtract
-                    )
-                else:
-                    nc.scalar.activation(out=dst, in_=src, func=ACT.Relu, bias=negb[:], scale=1.0)
+        for jj in range(PACK):
+            tb = t_banks[jj][:].bitcast(BF16)
+            src = tb[:, 0:512].rearrange("p (u m e) -> p m u e", u=2, e=2)
+            dst = a_sb[:, jj * 512 : (jj + 1) * 512].rearrange("p (m u e) -> p m u e", u=2, e=2)
+            if jj == 0:
+                nc.vector.tensor_scalar(
+                    out=dst, in0=src, scalar1=BOUND_GAMMA, scalar2=BOUND_GAMMA, op0=ALU.max, op1=ALU.subtract
+                )
+            else:
+                nc.scalar.activation(out=dst, in_=src, func=ACT.Relu, bias=negb[:], scale=1.0)
         for half in range(2):
             cols = slice(half * 1024, (half + 1) * 1024)
             nc.vector.scalar_tensor_tensor(

import concourse.mybir as mybir
from concourse.masks import make_identity

FLOPS = 2 * 512 * 512 * 2 * 4096

F32 = mybir.dt.float32
BF16 = mybir.dt.bfloat16
U32 = mybir.dt.uint32
U8 = mybir.dt.uint8
FP8X4 = mybir.dt.float8_e4m3fn_x4
ALU = mybir.AluOpType
ACT = mybir.ActivationFunctionType

P = 128
PACK = 4
PIX = 4096
CHUNK = 512
N_CHUNKS = 2 * PIX // CHUNK
SQUARE_LEAD = 3
S_LEAD = 4
QUANT_LEAD = 2
FINE_CHUNKS = 4
COARSE = N_CHUNKS - FINE_CHUNKS
XP = 216
G_COLS = 168

S_COLS = (296,) * 3 + (228,) * 10 + (296, 296, 512)

PEDESTAL = 2.0 ** -36
BOUND_GAMMA = 2.0 ** -18
BOUND_BETA = (1e-6 + PEDESTAL) ** 0.5

LOADS = (
    (0, 0, 512),
    (0, 512, 512),
    (0, 1024, 512),
    (0, 1536, 512),
    (0, 2048, 1024),
    (0, 3072, 1024),
    (1, 0, 2048),
    (1, 2048, 2048),
)


def tile_einsumgdn_kernel(tc, x, beta, gamma, out):
    nc = tc.nc
    xv = x.rearrange("n (p j) h w -> n p j (h w)", j=PACK)
    ov = out.rearrange("n (p j) h w -> n p j (h w)", j=PACK)

    with tc.tile_pool(name="keep", bufs=1) as keep, tc.tile_pool(name="work", bufs=6) as work, tc.tile_pool(
        name="res", bufs=6
    ) as res, tc.tile_pool(name="res2", bufs=2) as res2, tc.psum_pool(name="psum", bufs=4) as psum, tc.manual_schedule():
        x_tiles = []
        for i, (n, p0, width) in enumerate(LOADS):
            xt = keep.tile([P, PACK, width], BF16, name="x%d" % i, tag="x%d" % i)
            x_tiles.append(xt)
        g_sb = keep.tile([P, PACK * 512], BF16)
        b_sb = keep.tile([P, PACK], BF16)

        def load_x(i):
            n, p0, width = LOADS[i]
            nc.sync.dma_start(out=x_tiles[i][:], in_=xv[n, :, :, p0 : p0 + width])

        load_x(0)
        nc.sync.dma_start(out=g_sb[:], in_=gamma.rearrange("(m j) c -> m (j c)", j=PACK))
        nc.sync.dma_start(out=b_sb[:], in_=beta.rearrange("(p j) -> p j", j=PACK))
        for i in range(1, len(LOADS)):
            load_x(i)

        def where(k):
            n = k // (PIX // CHUNK)
            p0 = (k % (PIX // CHUNK)) * CHUNK
            for i, (ln, lp, lw) in enumerate(LOADS):
                if ln == n and lp <= p0 and p0 + CHUNK <= lp + lw:
                    return x_tiles[i], p0 - lp, n, p0
            raise ValueError("chunk outside the loads")

        one = keep.tile([P, 1], F32)
        nc.vector.memset(one[:], 1.0)
        negb = keep.tile([P, 1], F32)
        nc.vector.memset(negb[:], -BOUND_GAMMA)
        warm = keep.tile([P, 1], F32)
        nc.scalar.activation(out=warm[:], in_=one[:], func=ACT.Abs_reciprocal_sqrt)
        ident_bf = keep.tile([P, P], BF16)
        make_identity(nc, ident_bf[:])
        ident = keep.tile([P, P], F32)
        make_identity(nc, ident[:])

        grouped = {}
        codes = {}
        planes = {}
        results = {}
        pairs = {}
        banks = {}
        x_psum = {}

        def copy_to_psum(k):
            if k >= N_CHUNKS or S_COLS[k] == CHUNK:
                return
            xt, off, n, p0 = where(k)
            xp = psum.tile([P, PACK, 256], BF16, name="xp", tag="xp")
            x_psum[k] = xp
            for jj in range(PACK):
                nc.tensor.matmul(
                    out=xp[:, jj, 0:XP], lhsT=ident_bf[:], rhs=xt[:, jj, off : off + XP], start=True, stop=True
                )

        def square_views(k, w0, w1):
            xt, off, n, p0 = where(k)
            if k not in grouped:
                gq = work.tile([P, CHUNK, PACK], BF16, align_bytes=64, name="gq", tag="gq")
                grouped[k] = gq
            dst = grouped[k][:, w0:w1, :].rearrange("p (c i) t -> p c t i", i=4)
            src = xt[:, :, off + w0 : off + w1].rearrange("p t (c i) -> p c t i", i=4)
            return dst, src

        def square_scalar(k):
            if k < N_CHUNKS:
                dst, src = square_views(k, CHUNK - S_COLS[k], CHUNK)
                nc.scalar.activation(out=dst, in_=src, func=ACT.Square)

        def square_vector(k):
            if k < N_CHUNKS and XP + S_COLS[k] < CHUNK:
                dst, src = square_views(k, XP, CHUNK - S_COLS[k])
                nc.vector.tensor_tensor(out=dst, in0=src, in1=src, op=ALU.mult)

        def square_psum(k):
            if k < N_CHUNKS and S_COLS[k] < CHUNK:
                dst, src = square_views(k, 0, XP)
                src_psum = x_psum[k][:, :, 0:XP].rearrange("p t (c i) -> p c t i", i=4)
                nc.vector.tensor_tensor(out=dst, in0=src_psum, in1=src, op=ALU.mult)

        def quantise(k):
            if k >= N_CHUNKS:
                return
            cw = keep.tile([P, CHUNK], U32, align_bytes=64, name="cw%d" % k, tag="cw%d" % k)
            sp = keep.tile([P, CHUNK], U8, align_bytes=64, name="sp%d" % k, tag="sp%d" % k)
            codes[k] = cw
            planes[k] = sp
            nc.vector.quantize_mx(
                out=cw[:].bitcast(FP8X4), scales=sp[:], in_=grouped[k][:].rearrange("p w t -> p (w t)")
            )

        def pass_one(k, jj):
            acc = psum.tile([P, CHUNK], F32, name="bank", tag="bank")
            banks[(k, jj)] = acc
            nc.tensor.matmul_mx(
                out=acc[:],
                lhsT=g_codes[:, jj * P : (jj + 1) * P].bitcast(FP8X4),
                lhsT_scale=g_plane[:, jj * P : (jj + 1) * P],
                rhs=codes[k][:].bitcast(FP8X4),
                rhs_scale=planes[k][:],
                start=True,
                stop=True,
            )

        def passes(k):
            for jj in range(PACK):
                pass_one(k, jj)

        copy_to_psum(0)
        square_scalar(0)
        dst0, src0 = square_views(0, 0, CHUNK - S_COLS[0])
        nc.vector.tensor_tensor(out=dst0, in0=src0, in1=src0, op=ALU.mult)

        gw = g_sb[:].bitcast(F32)
        a_sb = keep.tile([P, PACK * 512], F32)
        g_eff = keep.tile([P, PACK * 512], BF16, align_bytes=64)
        t_banks = []
        for jj in range(PACK):
            tp = psum.tile([P, 512], F32, name="bank", tag="bank")
            t_banks.append(tp)
            for u in range(2):
                nc.tensor.transpose(
                    tp[:, u * P : (u + 1) * P],
                    gw[:, jj * 256 + u : (jj + 1) * 256 : 2],
                    ident[:],
                )
        copy_to_psum(1)
        copy_to_psum(2)

        b_max = keep.tile([P, PACK], F32)
        nc.gpsimd.tensor_scalar(out=b_max[:], in0=b_sb[:], scalar1=BOUND_BETA, scalar2=None, op0=ALU.max)
        b_sq = keep.tile([P, PACK], F32)
        nc.gpsimd.tensor_tensor(out=b_sq[:], in0=b_max[:], in1=b_max[:], op=ALU.mult)
        b_eff = keep.tile([P, PACK], F32)
        nc.gpsimd.tensor_scalar(out=b_eff[:], in0=b_sq[:], scalar1=PEDESTAL, scalar2=None, op0=ALU.subtract)

        quantise(0)

        for jj in range(PACK):
            tb = t_banks[jj][:].bitcast(BF16)
            src = tb[:, 0:512].rearrange("p (u m e) -> p m u e", u=2, e=2)
            dst = a_sb[:, jj * 512 : (jj + 1) * 512].rearrange("p (m u e) -> p m u e", u=2, e=2)
            if jj == 0:
                nc.vector.tensor_scalar(
                    out=dst, in0=src, scalar1=BOUND_GAMMA, scalar2=BOUND_GAMMA, op0=ALU.max, op1=ALU.subtract
                )
            else:
                nc.scalar.activation(out=dst, in_=src, func=ACT.Relu, bias=negb[:], scale=1.0)
        for half in range(2):
            cols = slice(half * 1024, (half + 1) * 1024)
            nc.vector.scalar_tensor_tensor(
                out=g_eff[:, cols],
                in0=a_sb[:, cols],
                scalar=2.0 * BOUND_GAMMA,
                in1=a_sb[:, cols],
                op0=ALU.add,
                op1=ALU.mult,
            )
        square_scalar(1)
        g_codes = keep.tile([P, 512], U32, align_bytes=64)
        g_plane = keep.tile([P, 512], U8, align_bytes=64)
        nc.vector.quantize_mx(out=g_codes[:].bitcast(FP8X4), scales=g_plane[:], in_=g_eff[:])
        passes(0)
        square_scalar(2)
        square_scalar(3)
        square_vector(1)
        square_psum(1)
        quantise(1)
        square_vector(2)
        square_psum(2)

        def rsqrt(k, jj, w0=0, w1=CHUNK):
            if jj == 0 and k < COARSE:
                r = res.tile([P, PACK, CHUNK], F32, name="r", tag="r")
                results[k] = r
            if jj == 0 and k >= COARSE and k % 2 == 0:
                two = res2.tile([P, PACK, 2 * CHUNK], F32, name="two", tag="two")
                pairs[k] = two
                results[k] = two[:, :, 0:CHUNK]
                results[k + 1] = two[:, :, CHUNK : 2 * CHUNK]
            nc.scalar.activation(
                out=results[k][:, jj, w0:w1],
                in_=banks[(k, jj)][:, w0:w1],
                func=ACT.Abs_reciprocal_sqrt,
                bias=b_eff[:, jj : jj + 1],
                scale=1.0,
            )

        def product(engine, k, j0, j1, w0, w1):
            xt, off, n, p0 = where(k)
            r = results[k][:, j0:j1, w0:w1]
            engine.tensor_tensor(out=r, in0=r, in1=xt[:, j0:j1, off + w0 : off + w1], op=ALU.mult)

        def product_psum(k):
            r = results[k][:, :, 0:XP]
            nc.vector.tensor_tensor(out=r, in0=x_psum[k][:, :, 0:XP], in1=r, op=ALU.mult)

        def store(k, j0, j1, w0=0, w1=CHUNK):
            xt, off, n, p0 = where(k)
            nc.sync.dma_start(out=ov[n, :, j0:j1, p0 + w0 : p0 + w1], in_=results[k][:, j0:j1, w0:w1])

        def product_two(k, jj):
            xt, off, n, p0 = where(k)
            r = pairs[k][:, jj, :]
            nc.vector.tensor_tensor(out=r, in0=r, in1=xt[:, jj, off : off + 2 * CHUNK], op=ALU.mult)
            nc.sync.dma_start(out=ov[n, :, jj, p0 : p0 + 2 * CHUNK], in_=r)

        units = [(first + h, jj) for first in range(COARSE, N_CHUNKS, 2) for jj in range(PACK) for h in (0, 1)]

        for k in range(COARSE):
            copy_to_psum(k + SQUARE_LEAD)
            for jj in range(PACK):
                rsqrt(k, jj)
            if k + 1 < COARSE:
                passes(k + 1)
            square_scalar(k + S_LEAD)
            product(nc.vector, k, 0, 2, XP, CHUNK - G_COLS)
            quantise(k + QUANT_LEAD)
            if k + 1 == COARSE:
                for unit in units[0:4]:
                    pass_one(unit[0], unit[1])
            product(nc.vector, k, 2, 4, XP, CHUNK - G_COLS)
            product(nc.gpsimd, k, 0, 4, CHUNK - G_COLS, CHUNK)
            product_psum(k)
            square_psum(k + SQUARE_LEAD)
            square_vector(k + SQUARE_LEAD)
            store(k, 0, 4)
        for late in range(COARSE + QUANT_LEAD, N_CHUNKS):
            quantise(late)

        for i, (k, jj) in enumerate(units):
            end = k >= N_CHUNKS - 2 and jj == PACK - 1
            for w0, w1 in ((0, 256), (256, CHUNK)) if i == len(units) - 1 else ((0, CHUNK),):
                rsqrt(k, jj, w0, w1)
                if end:
                    product(nc.vector, k, jj, jj + 1, w0, w1)
                    store(k, jj, jj + 1, w0, w1)
            if i + 4 < len(units):
                pass_one(units[i + 4][0], units[i + 4][1])
            if k % 2 == 1 and not end:
                product_two(k - 1, jj)
